import numpy as np
import ml_dtypes


def mxq(x, axis, fmt="e4m3"):
    dtype, down = {"e4m3": (ml_dtypes.float8_e4m3fn, 7), "e5m2": (ml_dtypes.float8_e5m2, 14)}[fmt]
    v = np.moveaxis(np.asarray(x, np.float32).astype(ml_dtypes.bfloat16).astype(np.float64), axis, -1)
    blocks = v.reshape(v.shape[:-1] + (-1, 32))
    amax = np.abs(blocks).max(-1, keepdims=True)
    byte = np.maximum(np.where(amax > 0, np.frexp(amax)[1] - 1 + 127, 0) - down, 1)
    scale = np.exp2(byte - 127.0)
    codes = (blocks / scale).astype(np.float32).astype(dtype).astype(np.float64)
    return np.moveaxis((codes * scale).reshape(v.shape), -1, axis)


WIDE = False


def mx_kscale(k):
    if not WIDE:
        return np.ones(k)
    levels = np.array([20, -20, 10, -10, 0])
    a = np.random.permutation(np.resize(levels, k // 512 * 4)).reshape(k // 512, 4)
    idx = np.arange(k)
    return np.exp2(a[idx // 512, idx % 128 // 32])


BF16 = ml_dtypes.bfloat16


def bf(x):
    return np.asarray(x, np.float32).astype(BF16)


def f64(x):
    return np.asarray(x).astype(np.float64)


B, D_IN, H = 512, 512, 1024


def sigmoid(v):
    return 1.0 / (1.0 + np.exp(-v))


def setup_inputs():
    u = mx_kscale(H)
    inp = {"x": bf(np.random.standard_normal((B, D_IN))),
           "hidden_memory_tm1": bf(np.random.standard_normal((B, 2 * H))),
           "hidden_memory_tm2": bf(np.random.standard_normal((B, 2 * H)))}
    for g in "ifoc":
        inp["W" + g] = bf(np.random.standard_normal((D_IN, H)) * 0.6 / np.sqrt(D_IN))
        inp["U" + g] = bf(np.random.standard_normal((H, H)) * 0.6 / np.sqrt(H))
        inp["V" + g] = bf(np.random.standard_normal((H, H)) * 0.6 / np.sqrt(H))
    go = np.random.standard_normal((B, 2 * H)) * np.exp2(np.random.randint(-12, 1, (B, 1))) * 16.0
    W0 = np.concatenate([f64(inp["W" + g]) for g in "ifoc"], axis=1)
    U0 = np.concatenate([f64(inp["U" + g]) for g in "ifoc"], axis=1)
    V0 = np.concatenate([f64(inp["V" + g]) for g in "ifoc"], axis=1)
    gates = (f64(inp["x"]) @ W0
             + f64(inp["hidden_memory_tm1"])[:, :H] @ U0
             + f64(inp["hidden_memory_tm2"])[:, :H] @ V0)
    for g in "ifoc":
        inp["W" + g] = bf(f64(inp["W" + g]) / u[None, :])
    inp["gates"] = np.asarray(gates, np.float32)
    inp["grad_out"] = bf(go * np.concatenate([u, u])[None, :])
    return inp


def reference(x, hidden_memory_tm1, hidden_memory_tm2, Wi, Ui, Vi, Wf, Uf, Vf, Wo, Uo, Vo, Wc, Uc, Vc, gates, grad_out):
    a = f64(gates)
    g = f64(grad_out)
    c_prev = f64(hidden_memory_tm1)[:, H:]
    i = sigmoid(a[:, 0 * H:1 * H])
    f = sigmoid(a[:, 1 * H:2 * H])
    o = sigmoid(a[:, 2 * H:3 * H])
    c_ = np.tanh(a[:, 3 * H:4 * H])
    c = f * c_prev + i * c_
    tc = np.tanh(c)
    dh = g[:, :H]
    dc = g[:, H:] + dh * o * (1.0 - tc * tc)
    da = np.concatenate([dc * c_ * i * (1.0 - i),
                         dc * c_prev * f * (1.0 - f),
                         dh * tc * o * (1.0 - o),
                         dc * i * (1.0 - c_ * c_)], axis=1)
    W = np.concatenate([f64(Wi), f64(Wf), f64(Wo), f64(Wc)], axis=1)
    return mxq(da, 1, "e5m2") @ mxq(W, 1, "e4m3").T

@@ -1,0 +1,225 @@
+from contextlib import ExitStack
+
+import concourse.mybir as mybir
+from concourse.masks import make_identity
+
+F32 = mybir.dt.float32
+BF16 = mybir.dt.bfloat16
+U32 = mybir.dt.uint32
+U8 = mybir.dt.uint8
+E4M3_X4 = mybir.dt.float8_e4m3fn_x4
+E5M2_X4 = mybir.dt.float8_e5m2_x4
+FUNC = mybir.ActivationFunctionType
+ALU = mybir.AluOpType
+
+P = 128
+PACK = 4
+K_PASS = P * PACK
+
+BATCH, D_IN, HIDDEN = 512, 512, 1024
+GATE_I, GATE_F, GATE_O, GATE_C = 0, 1, 2, 3
+N_GATES = 4
+N_HALVES = HIDDEN // K_PASS
+N_CHUNKS = (BATCH // P) * N_HALVES
+D_TILES = D_IN // P
+
+FLOPS = 2 * BATCH * D_IN * N_GATES * HIDDEN
+BYTES = 4 * BATCH * N_GATES * HIDDEN + 2 * BATCH * 3 * HIDDEN + 2 * D_IN * N_GATES * HIDDEN + 4 * BATCH * D_IN
+
+
+def dram_order(ap):
+    return ap.rearrange("p n (u q e) -> p (n u) e q", u=2, e=2)
+
+
+def on_chip_order(ap):
+    return ap.rearrange("p n (u e q) -> p (n u) e q", u=2, e=2)
+
+
+def value_last(bank):
+    return bank.rearrange("p t b -> p b t")
+
+
+def tile_bilaterallstmcell_v_kernel(
+    tc, x, hidden_memory_tm1, hidden_memory_tm2,
+    Wi, Ui, Vi, Wf, Uf, Vf, Wo, Uo, Vo, Wc, Uc, Vc,
+    gates, grad_out, out,
+):
+    nc = tc.nc
+    weights = (Wi, Wf, Wo, Wc)
+
+    with ExitStack() as stack:
+        stack.enter_context(tc.manual_schedule())
+        keep = stack.enter_context(tc.tile_pool(name="keep", bufs=1))
+        loaded = stack.enter_context(tc.tile_pool(name="loaded", bufs=3))
+        work = stack.enter_context(tc.tile_pool(name="work", bufs=2))
+        banks = stack.enter_context(tc.psum_pool(name="banks", bufs=6))
+        sums = stack.enter_context(tc.psum_pool(name="sums", bufs=2))
+
+        n_pass = N_GATES * N_HALVES
+        w_rows = keep.tile([P, n_pass, D_TILES, K_PASS], BF16)
+        w_grouped = keep.tile([P, n_pass, D_IN * PACK], BF16, align_bytes=64)
+        w_codes = keep.tile([P, n_pass, D_IN], U32, align_bytes=64)
+        w_scales = keep.tile([P, n_pass, D_IN], U8, align_bytes=64)
+
+        def load_chunk(n):
+            b_tile, half = divmod(n, N_HALVES)
+            rows = slice(b_tile * P, (b_tile + 1) * P)
+            cols = slice(half * K_PASS, (half + 1) * K_PASS)
+            pre = loaded.tile([P, N_GATES, K_PASS], F32, name="pre")
+            nc.sync.dma_start(out=pre[:], in_=gates[rows, :].rearrange("b (g h) -> b g h", g=N_GATES)[:, :, cols])
+            given = loaded.tile([P, 3, K_PASS], BF16, name="given")
+            nc.sync.dma_start(out=given[:, 0, :], in_=hidden_memory_tm1[rows, HIDDEN + half * K_PASS : HIDDEN + (half + 1) * K_PASS])
+            nc.sync.dma_start(out=given[:, 1:3, :], in_=grad_out[rows, :].rearrange("b (s h) -> b s h", s=2)[:, :, cols])
+            return pre, given
+
+        def load_weights(half):
+            cols = slice(half * K_PASS, (half + 1) * K_PASS)
+            for gate in range(N_GATES):
+                nc.sync.dma_start(
+                    out=w_rows[:, N_HALVES * gate + half],
+                    in_=weights[gate].rearrange("(j p) h -> p j h", p=P)[:, :, cols],
+                )
+
+        def transpose_weights(ps):
+            words = w_rows[:, ps].bitcast(F32)
+            grouped_words = w_grouped[:, ps].bitcast(F32).rearrange("p (d u) -> p d u", u=2)
+            for d_half in range(2):
+                bank = banks.tile([P, 2, 2 * P], F32, name="w_bank", tag="bank")
+                for u in range(2):
+                    for j in range(2):
+                        nc.tensor.transpose(
+                            out=bank[:, u, j * P : (j + 1) * P],
+                            in_=words[:, 2 * d_half + j, u * P : (u + 1) * P],
+                            identity=ident[:],
+                        )
+                nc.scalar.copy(
+                    out=grouped_words[:, d_half * 2 * P : (d_half + 1) * 2 * P, :],
+                    in_=bank[:].rearrange("p u d -> p d u"),
+                )
+
+        def quantise_weights(ps):
+            nc.vector.quantize_mx(out=w_codes[:, ps].bitcast(E4M3_X4), scales=w_scales[:, ps], in_=w_grouped[:, ps])
+
+        def gate_values(pre):
+            sig = work.tile([P, 3, K_PASS], F32, name="sig")
+            nc.scalar.activation(out=on_chip_order(sig[:]), in_=dram_order(pre[:, GATE_I : GATE_O + 1, :]), func=FUNC.Sigmoid)
+            cand = work.tile([P, 1, K_PASS], F32, name="cand")
+            nc.scalar.activation(out=on_chip_order(cand[:]), in_=dram_order(pre[:, GATE_C : GATE_C + 1, :]), func=FUNC.Tanh)
+            cand_sq = work.tile([P, K_PASS], F32, name="cand_sq")
+            nc.scalar.activation(out=cand_sq[:], in_=cand[:, 0, :], func=FUNC.Square)
+            return sig, cand, cand_sq
+
+        def transposed(rows_ap, name):
+            bank = banks.tile([P, PACK, P], F32, name=name, tag="bank")
+            for t in range(PACK):
+                nc.tensor.transpose(out=bank[:, t, :], in_=rows_ap[:, t * P : (t + 1) * P], identity=ident[:])
+            return bank
+
+        chunk_inputs = {0: load_chunk(0)}
+        load_weights(0)
+        chunk_inputs[1] = load_chunk(1)
+        load_weights(1)
+
+        ident = keep.tile([P, P], F32)
+        make_identity(nc, ident[:])
+
+        values = gate_values(chunk_inputs[0][0])
+        acc = None
+
+        for n in range(N_CHUNKS):
+            b_tile, half = divmod(n, N_HALVES)
+            given = chunk_inputs[n][1]
+            sig, cand, cand_sq = values
+            if n + 2 < N_CHUNKS:
+                chunk_inputs[n + 2] = load_chunk(n + 2)
+
+            if n < N_HALVES:
+                for gate in range(N_GATES):
+                    transpose_weights(N_HALVES * gate + n)
+
+            prod = work.tile([P, 3, K_PASS], F32, name="prod")
+            nc.vector.tensor_tensor(out=prod[:, 0, :], in0=sig[:, GATE_I, :], in1=cand[:, 0, :], op=ALU.mult)
+            nc.vector.tensor_tensor(
+                out=on_chip_order(prod[:, 1:3, :]), in0=on_chip_order(sig[:, GATE_F : GATE_O + 1, :]),
+                in1=dram_order(given[:, 0:2, :]), op=ALU.mult,
+            )
+            cell = work.tile([P, K_PASS], F32, name="cell")
+            nc.vector.tensor_tensor(out=cell[:], in0=prod[:, 0, :], in1=prod[:, 1, :], op=ALU.add)
+
+            dcs_words = given[:, 2, :].bitcast(F32)
+            dcs_bank = banks.tile([P, 2, P], F32, name="dcs_bank", tag="bank")
+            for u in range(2):
+                nc.tensor.transpose(out=dcs_bank[:, u, :], in_=dcs_words[:, u * P : (u + 1) * P], identity=ident[:])
+            cell_bank = transposed(cell, "cell_bank")
+            u_bank = transposed(prod[:, 2, :], "u_bank")
+
+            neg_tanh_c = work.tile([P, P, PACK], F32, name="neg_tanh_c")
+            nc.scalar.activation(out=neg_tanh_c[:], in_=value_last(cell_bank[:]), func=FUNC.Tanh, scale=-1.0)
+            tanh_c_sq = work.tile([P, P, PACK], F32, name="tanh_c_sq")
+            nc.scalar.activation(out=tanh_c_sq[:], in_=neg_tanh_c[:], func=FUNC.Square)
+
+            r = work.tile([P, N_GATES, K_PASS], F32, name="r")
+            nc.vector.scalar_tensor_tensor(
+                out=r[:, GATE_I : GATE_O + 1, :], in0=sig[:], scalar=1.0, in1=prod[:], op0=ALU.subtract, op1=ALU.mult
+            )
+            nc.vector.scalar_tensor_tensor(
+                out=r[:, GATE_C, :], in0=cand_sq[:], scalar=1.0, in1=sig[:, GATE_I, :], op0=ALU.subtract, op1=ALU.mult
+            )
+            r_bank = {}
+            for gate in (GATE_O, GATE_I, GATE_F, GATE_C):
+                r_bank[gate] = transposed(r[:, gate, :], "r_bank")
+
+            if n + 1 < N_CHUNKS:
+                values = gate_values(chunk_inputs[n + 1][0])
+
+            if n < N_HALVES:
+                for gate in range(N_GATES):
+                    quantise_weights(N_HALVES * gate + n)
+
+            da_grouped = work.tile([P, N_GATES, P, PACK], BF16, name="da_grouped", align_bytes=64)
+            da_codes = work.tile([P, N_GATES, P], U32, name="da_codes", align_bytes=64)
+            da_scales = work.tile([P, N_GATES, P], U8, name="da_scales", align_bytes=64)
+            if half == 0:
+                acc = sums.tile([P, D_IN], F32, name="acc")
+
+            def finish(gate, factor):
+                nc.vector.tensor_tensor(out=da_grouped[:, gate], in0=value_last(r_bank[gate][:]), in1=factor[:], op=ALU.mult)
+
+            def quantise_and_multiply(gate, first, last):
+                nc.vector.quantize_mx(
+                    out=da_codes[:, gate].bitcast(E5M2_X4),
+                    scales=da_scales[:, gate],
+                    in_=da_grouped[:, gate].rearrange("p b t -> p (b t)"),
+                )
+                ps = N_HALVES * gate + half
+                nc.tensor.matmul_mx(
+                    out=acc[:],
+                    lhsT=da_codes[:, gate].bitcast(E5M2_X4), lhsT_scale=da_scales[:, gate],
+                    rhs=w_codes[:, ps].bitcast(E4M3_X4), rhs_scale=w_scales[:, ps],
+                    start=first, stop=last,
+                )
+
+            finish(GATE_O, neg_tanh_c)
+            v = work.tile([P, P, PACK], F32, name="v")
+            nc.vector.scalar_tensor_tensor(
+                out=v[:], in0=tanh_c_sq[:], scalar=1.0, in1=value_last(u_bank[:]), op0=ALU.subtract, op1=ALU.mult
+            )
+            neg_dc = work.tile([P, P, PACK], F32, name="neg_dc")
+            nc.vector.tensor_tensor(
+                out=neg_dc[:].rearrange("p b (u e) -> p b u e", e=2),
+                in0=v[:].rearrange("p b (u e) -> p b u e", e=2),
+                in1=dcs_bank[:].bitcast(BF16).rearrange("p u (b e) -> p b u e", e=2),
+                op=ALU.subtract,
+            )
+            finish(GATE_I, neg_dc)
+            quantise_and_multiply(GATE_O, first=(half == 0), last=False)
+            finish(GATE_F, neg_dc)
+            quantise_and_multiply(GATE_I, first=False, last=False)
+            finish(GATE_C, neg_dc)
+            quantise_and_multiply(GATE_F, first=False, last=False)
+            quantise_and_multiply(GATE_C, first=False, last=(half == N_HALVES - 1))
+
+            if half == N_HALVES - 1:
+                result = work.tile([P, D_IN], F32, name="result")
+                nc.scalar.copy(out=result[:], in_=acc[:])
+                nc.sync.dma_start(out=out[b_tile * P : (b_tile + 1) * P, :], in_=result[:])

@@ -19,9 +19,11 @@ K_PASS = P * PACK
 BATCH, D_IN, HIDDEN = 512, 512, 1024
 GATE_I, GATE_F, GATE_O, GATE_C = 0, 1, 2, 3
 N_GATES = 4
+GATE_ORDER = (GATE_O, GATE_I, GATE_F, GATE_C)
 N_HALVES = HIDDEN // K_PASS
-N_CHUNKS = (BATCH // P) * N_HALVES
 D_TILES = D_IN // P
+CHUNKS = [(2 * pair + j, half) for pair in range(BATCH // P // 2) for half in range(N_HALVES) for j in range(2)]
+N_CHUNKS = len(CHUNKS)
 
 FLOPS = 2 * BATCH * D_IN * N_GATES * HIDDEN
 BYTES = 4 * BATCH * N_GATES * HIDDEN + 2 * BATCH * 3 * HIDDEN + 2 * D_IN * N_GATES * HIDDEN + 4 * BATCH * D_IN
@@ -50,7 +52,6 @@ def tile_bilaterallstmcell_v_kernel(
     with ExitStack() as stack:
         stack.enter_context(tc.manual_schedule())
         keep = stack.enter_context(tc.tile_pool(name="keep", bufs=1))
-        loaded = stack.enter_context(tc.tile_pool(name="loaded", bufs=3))
         work = stack.enter_context(tc.tile_pool(name="work", bufs=2))
         banks = stack.enter_context(tc.psum_pool(name="banks", bufs=6))
         sums = stack.enter_context(tc.psum_pool(name="sums", bufs=2))
@@ -60,27 +61,20 @@ def tile_bilaterallstmcell_v_kernel(
         w_grouped = keep.tile([P, n_pass, D_IN * PACK], BF16, align_bytes=64)
         w_codes = keep.tile([P, n_pass, D_IN], U32, align_bytes=64)
         w_scales = keep.tile([P, n_pass, D_IN], U8, align_bytes=64)
+        ident = keep.tile([P, P], F32)
 
-        def load_chunk(n):
-            b_tile, half = divmod(n, N_HALVES)
-            rows = slice(b_tile * P, (b_tile + 1) * P)
-            cols = slice(half * K_PASS, (half + 1) * K_PASS)
-            pre = loaded.tile([P, N_GATES, K_PASS], F32, name="pre")
-            nc.sync.dma_start(out=pre[:], in_=gates[rows, :].rearrange("b (g h) -> b g h", g=N_GATES)[:, :, cols])
-            given = loaded.tile([P, 3, K_PASS], BF16, name="given")
-            nc.sync.dma_start(out=given[:, 0, :], in_=hidden_memory_tm1[rows, HIDDEN + half * K_PASS : HIDDEN + (half + 1) * K_PASS])
-            nc.sync.dma_start(out=given[:, 1:3, :], in_=grad_out[rows, :].rearrange("b (s h) -> b s h", s=2)[:, :, cols])
-            return pre, given
+        pre, given, sig, cand, cand_sq, prod = {}, {}, {}, {}, {}, {}
+        u_bank, dcs_bank, neg_tanh_c, tanh_c_sq, r_bank, da_grouped, acc = {}, {}, {}, {}, {}, {}, {}
 
         def load_weights(half):
             cols = slice(half * K_PASS, (half + 1) * K_PASS)
-            for gate in range(N_GATES):
+            for gate in GATE_ORDER:
                 nc.sync.dma_start(
                     out=w_rows[:, N_HALVES * gate + half],
                     in_=weights[gate].rearrange("(j p) h -> p j h", p=P)[:, :, cols],
                 )
 
-        def transpose_weights(ps):
+        def regroup_weights(ps):
             words = w_rows[:, ps].bitcast(F32)
             grouped_words = w_grouped[:, ps].bitcast(F32).rearrange("p (d u) -> p d u", u=2)
             for d_half in range(2):
@@ -100,14 +94,38 @@ def tile_bilaterallstmcell_v_kernel(
         def quantise_weights(ps):
             nc.vector.quantize_mx(out=w_codes[:, ps].bitcast(E4M3_X4), scales=w_scales[:, ps], in_=w_grouped[:, ps])
 
-        def gate_values(pre):
-            sig = work.tile([P, 3, K_PASS], F32, name="sig")
-            nc.scalar.activation(out=on_chip_order(sig[:]), in_=dram_order(pre[:, GATE_I : GATE_O + 1, :]), func=FUNC.Sigmoid)
-            cand = work.tile([P, 1, K_PASS], F32, name="cand")
-            nc.scalar.activation(out=on_chip_order(cand[:]), in_=dram_order(pre[:, GATE_C : GATE_C + 1, :]), func=FUNC.Tanh)
-            cand_sq = work.tile([P, K_PASS], F32, name="cand_sq")
-            nc.scalar.activation(out=cand_sq[:], in_=cand[:, 0, :], func=FUNC.Square)
-            return sig, cand, cand_sq
+        def load_chunk(n):
+            b_tile, half = CHUNKS[n]
+            rows = slice(b_tile * P, (b_tile + 1) * P)
+            cols = slice(half * K_PASS, (half + 1) * K_PASS)
+            pre[n] = work.tile([P, N_GATES, K_PASS], F32, name="pre", bufs=3)
+            nc.sync.dma_start(out=pre[n][:], in_=gates[rows, :].rearrange("b (g h) -> b g h", g=N_GATES)[:, :, cols])
+            given[n] = work.tile([P, 3, K_PASS], BF16, name="given", bufs=4)
+            nc.sync.dma_start(
+                out=given[n][:, 0, :], in_=hidden_memory_tm1[rows, HIDDEN + half * K_PASS : HIDDEN + (half + 1) * K_PASS]
+            )
+            nc.sync.dma_start(out=given[n][:, 1:3, :], in_=grad_out[rows, :].rearrange("b (s h) -> b s h", s=2)[:, :, cols])
+
+        def gate_values(n):
+            sig[n] = work.tile([P, 3, K_PASS], F32, name="sig", bufs=3)
+            nc.scalar.activation(
+                out=on_chip_order(sig[n][:]), in_=dram_order(pre[n][:, GATE_I : GATE_O + 1, :]), func=FUNC.Sigmoid
+            )
+            cand[n] = work.tile([P, 1, K_PASS], F32, name="cand", bufs=3)
+            nc.scalar.activation(
+                out=on_chip_order(cand[n][:]), in_=dram_order(pre[n][:, GATE_C : GATE_C + 1, :]), func=FUNC.Tanh
+            )
+            cand_sq[n] = work.tile([P, K_PASS], F32, name="cand_sq", bufs=3)
+            nc.scalar.activation(out=cand_sq[n][:], in_=cand[n][:, 0, :], func=FUNC.Square)
+
+        def products(n, engine):
+            prod[n] = work.tile([P, 3, K_PASS], F32, name="prod", bufs=1)
+            engine.tensor_tensor(out=prod[n][:, 0, :], in0=sig[n][:, GATE_I, :], in1=cand[n][:, 0, :], op=ALU.mult)
+            for j, gate in ((1, GATE_F), (2, GATE_O)):
+                engine.tensor_tensor(
+                    out=on_chip_order(prod[n][:, j : j + 1, :]), in0=on_chip_order(sig[n][:, gate : gate + 1, :]),
+                    in1=dram_order(given[n][:, j - 1 : j, :]), op=ALU.mult,
+                )
 
         def transposed(rows_ap, name):
             bank = banks.tile([P, PACK, P], F32, name=name, tag="bank")
@@ -115,111 +133,111 @@ def tile_bilaterallstmcell_v_kernel(
                 nc.tensor.transpose(out=bank[:, t, :], in_=rows_ap[:, t * P : (t + 1) * P], identity=ident[:])
             return bank
 
-        chunk_inputs = {0: load_chunk(0)}
-        load_weights(0)
-        chunk_inputs[1] = load_chunk(1)
-        load_weights(1)
-
-        ident = keep.tile([P, P], F32)
-        make_identity(nc, ident[:])
-
-        values = gate_values(chunk_inputs[0][0])
-        acc = None
-
-        for n in range(N_CHUNKS):
-            b_tile, half = divmod(n, N_HALVES)
-            given = chunk_inputs[n][1]
-            sig, cand, cand_sq = values
-            if n + 2 < N_CHUNKS:
-                chunk_inputs[n + 2] = load_chunk(n + 2)
-
-            if n < N_HALVES:
-                for gate in range(N_GATES):
-                    transpose_weights(N_HALVES * gate + n)
-
-            prod = work.tile([P, 3, K_PASS], F32, name="prod")
-            nc.vector.tensor_tensor(out=prod[:, 0, :], in0=sig[:, GATE_I, :], in1=cand[:, 0, :], op=ALU.mult)
-            nc.vector.tensor_tensor(
-                out=on_chip_order(prod[:, 1:3, :]), in0=on_chip_order(sig[:, GATE_F : GATE_O + 1, :]),
-                in1=dram_order(given[:, 0:2, :]), op=ALU.mult,
-            )
-            cell = work.tile([P, K_PASS], F32, name="cell")
-            nc.vector.tensor_tensor(out=cell[:], in0=prod[:, 0, :], in1=prod[:, 1, :], op=ALU.add)
-
-            dcs_words = given[:, 2, :].bitcast(F32)
-            dcs_bank = banks.tile([P, 2, P], F32, name="dcs_bank", tag="bank")
+        def cell_state(n):
+            cell_bank = banks.tile([P, PACK, P], F32, name="cell_bank", tag="bank")
+            for t in range(PACK):
+                block = slice(t * P, (t + 1) * P)
+                nc.tensor.matmul(out=cell_bank[:, t, :], lhsT=prod[n][:, 0, block], rhs=ident[:], is_transpose=True, start=True, stop=False)
+                nc.tensor.matmul(out=cell_bank[:, t, :], lhsT=prod[n][:, 1, block], rhs=ident[:], is_transpose=True, start=False, stop=True)
+            neg_tanh_c[n] = work.tile([P, P, PACK], F32, name="neg_tanh_c")
+            nc.scalar.activation(out=neg_tanh_c[n][:], in_=value_last(cell_bank[:]), func=FUNC.Tanh, scale=-1.0)
+            tanh_c_sq[n] = work.tile([P, P, PACK], F32, name="tanh_c_sq")
+            nc.scalar.activation(out=tanh_c_sq[n][:], in_=neg_tanh_c[n][:], func=FUNC.Square)
+            u_bank[n] = transposed(prod[n][:, 2, :], "u_bank")
+            dcs_words = given[n][:, 2, :].bitcast(F32)
+            dcs_bank[n] = banks.tile([P, 2, P], F32, name="dcs_bank", tag="bank")
             for u in range(2):
-                nc.tensor.transpose(out=dcs_bank[:, u, :], in_=dcs_words[:, u * P : (u + 1) * P], identity=ident[:])
-            cell_bank = transposed(cell, "cell_bank")
-            u_bank = transposed(prod[:, 2, :], "u_bank")
+                nc.tensor.transpose(out=dcs_bank[n][:, u, :], in_=dcs_words[:, u * P : (u + 1) * P], identity=ident[:])
 
-            neg_tanh_c = work.tile([P, P, PACK], F32, name="neg_tanh_c")
-            nc.scalar.activation(out=neg_tanh_c[:], in_=value_last(cell_bank[:]), func=FUNC.Tanh, scale=-1.0)
-            tanh_c_sq = work.tile([P, P, PACK], F32, name="tanh_c_sq")
-            nc.scalar.activation(out=tanh_c_sq[:], in_=neg_tanh_c[:], func=FUNC.Square)
-
+        def factors(n):
             r = work.tile([P, N_GATES, K_PASS], F32, name="r")
             nc.vector.scalar_tensor_tensor(
-                out=r[:, GATE_I : GATE_O + 1, :], in0=sig[:], scalar=1.0, in1=prod[:], op0=ALU.subtract, op1=ALU.mult
+                out=r[:, GATE_I : GATE_O + 1, :], in0=sig[n][:], scalar=1.0, in1=prod[n][:], op0=ALU.subtract, op1=ALU.mult
             )
             nc.vector.scalar_tensor_tensor(
-                out=r[:, GATE_C, :], in0=cand_sq[:], scalar=1.0, in1=sig[:, GATE_I, :], op0=ALU.subtract, op1=ALU.mult
+                out=r[:, GATE_C, :], in0=cand_sq[n][:], scalar=1.0, in1=sig[n][:, GATE_I, :], op0=ALU.subtract, op1=ALU.mult
             )
-            r_bank = {}
-            for gate in (GATE_O, GATE_I, GATE_F, GATE_C):
-                r_bank[gate] = transposed(r[:, gate, :], "r_bank")
+            r_bank[n] = {}
+            for gate in GATE_ORDER:
+                r_bank[n][gate] = transposed(r[:, gate, :], "r_bank")
 
-            if n + 1 < N_CHUNKS:
-                values = gate_values(chunk_inputs[n + 1][0])
-
-            if n < N_HALVES:
-                for gate in range(N_GATES):
-                    quantise_weights(N_HALVES * gate + n)
-
-            da_grouped = work.tile([P, N_GATES, P, PACK], BF16, name="da_grouped", align_bytes=64)
-            da_codes = work.tile([P, N_GATES, P], U32, name="da_codes", align_bytes=64)
-            da_scales = work.tile([P, N_GATES, P], U8, name="da_scales", align_bytes=64)
-            if half == 0:
-                acc = sums.tile([P, D_IN], F32, name="acc")
-
-            def finish(gate, factor):
-                nc.vector.tensor_tensor(out=da_grouped[:, gate], in0=value_last(r_bank[gate][:]), in1=factor[:], op=ALU.mult)
-
-            def quantise_and_multiply(gate, first, last):
-                nc.vector.quantize_mx(
-                    out=da_codes[:, gate].bitcast(E5M2_X4),
-                    scales=da_scales[:, gate],
-                    in_=da_grouped[:, gate].rearrange("p b t -> p (b t)"),
-                )
-                ps = N_HALVES * gate + half
-                nc.tensor.matmul_mx(
-                    out=acc[:],
-                    lhsT=da_codes[:, gate].bitcast(E5M2_X4), lhsT_scale=da_scales[:, gate],
-                    rhs=w_codes[:, ps].bitcast(E4M3_X4), rhs_scale=w_scales[:, ps],
-                    start=first, stop=last,
-                )
-
-            finish(GATE_O, neg_tanh_c)
+        def gradients(n):
+            da_grouped[n] = work.tile([P, N_GATES, P, PACK], BF16, name="da_grouped", align_bytes=64)
             v = work.tile([P, P, PACK], F32, name="v")
             nc.vector.scalar_tensor_tensor(
-                out=v[:], in0=tanh_c_sq[:], scalar=1.0, in1=value_last(u_bank[:]), op0=ALU.subtract, op1=ALU.mult
+                out=v[:], in0=tanh_c_sq[n][:], scalar=1.0, in1=value_last(u_bank[n][:]), op0=ALU.subtract, op1=ALU.mult
+            )
+            nc.vector.tensor_tensor(
+                out=da_grouped[n][:, GATE_O], in0=value_last(r_bank[n][GATE_O][:]), in1=neg_tanh_c[n][:], op=ALU.mult
             )
             neg_dc = work.tile([P, P, PACK], F32, name="neg_dc")
             nc.vector.tensor_tensor(
                 out=neg_dc[:].rearrange("p b (u e) -> p b u e", e=2),
                 in0=v[:].rearrange("p b (u e) -> p b u e", e=2),
-                in1=dcs_bank[:].bitcast(BF16).rearrange("p u (b e) -> p b u e", e=2),
+                in1=dcs_bank[n][:].bitcast(BF16).rearrange("p u (b e) -> p b u e", e=2),
                 op=ALU.subtract,
             )
-            finish(GATE_I, neg_dc)
-            quantise_and_multiply(GATE_O, first=(half == 0), last=False)
-            finish(GATE_F, neg_dc)
-            quantise_and_multiply(GATE_I, first=False, last=False)
-            finish(GATE_C, neg_dc)
-            quantise_and_multiply(GATE_F, first=False, last=False)
-            quantise_and_multiply(GATE_C, first=False, last=(half == N_HALVES - 1))
+            for gate in (GATE_I, GATE_F, GATE_C):
+                nc.vector.tensor_tensor(
+                    out=da_grouped[n][:, gate], in0=value_last(r_bank[n][gate][:]), in1=neg_dc[:], op=ALU.mult
+                )
 
+        def contract(n):
+            b_tile, half = CHUNKS[n]
+            da_codes = work.tile([P, N_GATES, P], U32, name="da_codes", align_bytes=64)
+            da_scales = work.tile([P, N_GATES, P], U8, name="da_scales", align_bytes=64)
+            if half == 0:
+                acc[b_tile] = sums.tile([P, D_IN], F32, name="acc")
+            for gate in GATE_ORDER:
+                nc.vector.quantize_mx(
+                    out=da_codes[:, gate].bitcast(E5M2_X4),
+                    scales=da_scales[:, gate],
+                    in_=da_grouped[n][:, gate].rearrange("p b t -> p (b t)"),
+                )
+            for gate in GATE_ORDER:
+                ps = N_HALVES * gate + half
+                nc.tensor.matmul_mx(
+                    out=acc[b_tile][:],
+                    lhsT=da_codes[:, gate].bitcast(E5M2_X4), lhsT_scale=da_scales[:, gate],
+                    rhs=w_codes[:, ps].bitcast(E4M3_X4), rhs_scale=w_scales[:, ps],
+                    start=(half == 0 and gate == GATE_ORDER[0]),
+                    stop=(half == N_HALVES - 1 and gate == GATE_ORDER[-1]),
+                )
             if half == N_HALVES - 1:
                 result = work.tile([P, D_IN], F32, name="result")
-                nc.scalar.copy(out=result[:], in_=acc[:])
+                nc.scalar.copy(out=result[:], in_=acc[b_tile][:])
                 nc.sync.dma_start(out=out[b_tile * P : (b_tile + 1) * P, :], in_=result[:])
+
+        load_weights(0)
+        for n in range(4):
+            load_chunk(n)
+        load_weights(1)
+        make_identity(nc, ident[:])
+        for gate in GATE_ORDER:
+            regroup_weights(N_HALVES * gate)
+            quantise_weights(N_HALVES * gate)
+        gate_values(0)
+        gate_values(1)
+        products(0, nc.vector)
+        cell_state(0)
+        gate_values(2)
+        factors(0)
+
+        for n in range(N_CHUNKS):
+            if n + 4 < N_CHUNKS:
+                load_chunk(n + 4)
+            if n + 1 < N_CHUNKS:
+                products(n + 1, nc.gpsimd)
+                cell_state(n + 1)
+            if n + 3 < N_CHUNKS:
+                gate_values(n + 3)
+            gradients(n)
+            if 1 <= n <= 2:
+                for gate in GATE_ORDER[2 * n - 2 : 2 * n]:
+                    quantise_weights(N_HALVES * gate + 1)
+            contract(n)
+            if n + 1 < N_CHUNKS:
+                factors(n + 1)
+            if n < 2:
+                for gate in GATE_ORDER[2 * n : 2 * n + 2]:
+                    regroup_weights(N_HALVES * gate + 1)

@@ -24,6 +24,11 @@ N_HALVES = HIDDEN // K_PASS
 D_TILES = D_IN // P
 CHUNKS = [(2 * pair + j, half) for pair in range(BATCH // P // 2) for half in range(N_HALVES) for j in range(2)]
 N_CHUNKS = len(CHUNKS)
+PASSES_BY_ROUND = (
+    tuple(N_HALVES * gate for gate in GATE_ORDER),
+    tuple(N_HALVES * gate + 1 for gate in GATE_ORDER[:2]),
+    tuple(N_HALVES * gate + 1 for gate in GATE_ORDER[2:]),
+)
 
 FLOPS = 2 * BATCH * D_IN * N_GATES * HIDDEN
 BYTES = 4 * BATCH * N_GATES * HIDDEN + 2 * BATCH * 3 * HIDDEN + 2 * D_IN * N_GATES * HIDDEN + 4 * BATCH * D_IN
@@ -64,7 +69,8 @@ def tile_bilaterallstmcell_v_kernel(
         ident = keep.tile([P, P], F32)
 
         pre, given, sig, cand, cand_sq, prod = {}, {}, {}, {}, {}, {}
-        u_bank, dcs_bank, neg_tanh_c, tanh_c_sq, r_bank, da_grouped, acc = {}, {}, {}, {}, {}, {}, {}
+        u_bank, dcs_bank, neg_tanh_c, tanh_c_sq, r_bank = {}, {}, {}, {}, {}
+        da_grouped, da_codes, da_scales, acc = {}, {}, {}, {}
 
         def load_weights(half):
             cols = slice(half * K_PASS, (half + 1) * K_PASS)
@@ -108,14 +114,20 @@ def tile_bilaterallstmcell_v_kernel(
 
         def gate_values(n):
             sig[n] = work.tile([P, 3, K_PASS], F32, name="sig", bufs=3)
-            nc.scalar.activation(
-                out=on_chip_order(sig[n][:]), in_=dram_order(pre[n][:, GATE_I : GATE_O + 1, :]), func=FUNC.Sigmoid
-            )
             cand[n] = work.tile([P, 1, K_PASS], F32, name="cand", bufs=3)
+            cand_sq[n] = work.tile([P, K_PASS], F32, name="cand_sq", bufs=3)
+
+            def sigmoid(gate):
+                nc.scalar.activation(
+                    out=on_chip_order(sig[n][:, gate : gate + 1, :]), in_=dram_order(pre[n][:, gate : gate + 1, :]), func=FUNC.Sigmoid
+                )
+
+            sigmoid(GATE_I)
             nc.scalar.activation(
                 out=on_chip_order(cand[n][:]), in_=dram_order(pre[n][:, GATE_C : GATE_C + 1, :]), func=FUNC.Tanh
             )
-            cand_sq[n] = work.tile([P, K_PASS], F32, name="cand_sq", bufs=3)
+            sigmoid(GATE_F)
+            sigmoid(GATE_O)
             nc.scalar.activation(out=cand_sq[n][:], in_=cand[n][:, 0, :], func=FUNC.Square)
 
         def products(n, engine):
@@ -161,8 +173,29 @@ def tile_bilaterallstmcell_v_kernel(
             for gate in GATE_ORDER:
                 r_bank[n][gate] = transposed(r[:, gate, :], "r_bank")
 
-        def gradients(n):
+        def contract(n, gate):
+            b_tile, half = CHUNKS[n]
+            nc.vector.quantize_mx(
+                out=da_codes[n][:, gate].bitcast(E5M2_X4),
+                scales=da_scales[n][:, gate],
+                in_=da_grouped[n][:, gate].rearrange("p b t -> p (b t)"),
+            )
+            ps = N_HALVES * gate + half
+            nc.tensor.matmul_mx(
+                out=acc[b_tile][:],
+                lhsT=da_codes[n][:, gate].bitcast(E5M2_X4), lhsT_scale=da_scales[n][:, gate],
+                rhs=w_codes[:, ps].bitcast(E4M3_X4), rhs_scale=w_scales[:, ps],
+                start=(half == 0 and gate == GATE_ORDER[0]),
+                stop=(half == N_HALVES - 1 and gate == GATE_ORDER[-1]),
+            )
+
+        def gradients(n, contract_at_once):
+            b_tile, half = CHUNKS[n]
             da_grouped[n] = work.tile([P, N_GATES, P, PACK], BF16, name="da_grouped", align_bytes=64)
+            da_codes[n] = work.tile([P, N_GATES, P], U32, name="da_codes", align_bytes=64)
+            da_scales[n] = work.tile([P, N_GATES, P], U8, name="da_scales", align_bytes=64)
+            if half == 0:
+                acc[b_tile] = sums.tile([P, D_IN], F32, name="acc")
             v = work.tile([P, P, PACK], F32, name="v")
             nc.vector.scalar_tensor_tensor(
                 out=v[:], in0=tanh_c_sq[n][:], scalar=1.0, in1=value_last(u_bank[n][:]), op0=ALU.subtract, op1=ALU.mult
@@ -177,51 +210,34 @@ def tile_bilaterallstmcell_v_kernel(
                 in1=dcs_bank[n][:].bitcast(BF16).rearrange("p u (b e) -> p b u e", e=2),
                 op=ALU.subtract,
             )
-            for gate in (GATE_I, GATE_F, GATE_C):
+            for k in range(1, N_GATES):
+                gate = GATE_ORDER[k]
                 nc.vector.tensor_tensor(
                     out=da_grouped[n][:, gate], in0=value_last(r_bank[n][gate][:]), in1=neg_dc[:], op=ALU.mult
                 )
+                if contract_at_once:
+                    contract(n, GATE_ORDER[k - 1])
 
-        def contract(n):
-            b_tile, half = CHUNKS[n]
-            da_codes = work.tile([P, N_GATES, P], U32, name="da_codes", align_bytes=64)
-            da_scales = work.tile([P, N_GATES, P], U8, name="da_scales", align_bytes=64)
-            if half == 0:
-                acc[b_tile] = sums.tile([P, D_IN], F32, name="acc")
-            for gate in GATE_ORDER:
-                nc.vector.quantize_mx(
-                    out=da_codes[:, gate].bitcast(E5M2_X4),
-                    scales=da_scales[:, gate],
-                    in_=da_grouped[n][:, gate].rearrange("p b t -> p (b t)"),
-                )
-            for gate in GATE_ORDER:
-                ps = N_HALVES * gate + half
-                nc.tensor.matmul_mx(
-                    out=acc[b_tile][:],
-                    lhsT=da_codes[:, gate].bitcast(E5M2_X4), lhsT_scale=da_scales[:, gate],
-                    rhs=w_codes[:, ps].bitcast(E4M3_X4), rhs_scale=w_scales[:, ps],
-                    start=(half == 0 and gate == GATE_ORDER[0]),
-                    stop=(half == N_HALVES - 1 and gate == GATE_ORDER[-1]),
-                )
-            if half == N_HALVES - 1:
-                result = work.tile([P, D_IN], F32, name="result")
-                nc.scalar.copy(out=result[:], in_=acc[b_tile][:])
-                nc.sync.dma_start(out=out[b_tile * P : (b_tile + 1) * P, :], in_=result[:])
+        def store(b_tile):
+            result = work.tile([P, D_IN], F32, name="result")
+            nc.scalar.copy(out=result[:], in_=acc[b_tile][:])
+            nc.sync.dma_start(out=out[b_tile * P : (b_tile + 1) * P, :], in_=result[:])
 
+        load_chunk(0)
+        load_chunk(1)
         load_weights(0)
-        for n in range(4):
-            load_chunk(n)
+        load_chunk(2)
+        load_chunk(3)
         load_weights(1)
         make_identity(nc, ident[:])
-        for gate in GATE_ORDER:
-            regroup_weights(N_HALVES * gate)
-            quantise_weights(N_HALVES * gate)
         gate_values(0)
         gate_values(1)
         products(0, nc.vector)
         cell_state(0)
-        gate_values(2)
         factors(0)
+        for ps in PASSES_BY_ROUND[0]:
+            regroup_weights(ps)
+        gate_values(2)
 
         for n in range(N_CHUNKS):
             if n + 4 < N_CHUNKS:
@@ -231,13 +247,17 @@ def tile_bilaterallstmcell_v_kernel(
                 cell_state(n + 1)
             if n + 3 < N_CHUNKS:
                 gate_values(n + 3)
-            gradients(n)
-            if 1 <= n <= 2:
-                for gate in GATE_ORDER[2 * n - 2 : 2 * n]:
-                    quantise_weights(N_HALVES * gate + 1)
-            contract(n)
+            last_round = n == N_CHUNKS - 1
+            gradients(n, contract_at_once=last_round)
+            if n < len(PASSES_BY_ROUND):
+                for ps in PASSES_BY_ROUND[n]:
+                    quantise_weights(ps)
+            for gate in GATE_ORDER[-1:] if last_round else GATE_ORDER:
+                contract(n, gate)
+            if CHUNKS[n][1] == N_HALVES - 1:
+                store(CHUNKS[n][0])
             if n + 1 < N_CHUNKS:
                 factors(n + 1)
-            if n < 2:
-                for gate in GATE_ORDER[2 * n : 2 * n + 2]:
-                    regroup_weights(N_HALVES * gate + 1)
+            if n + 1 < len(PASSES_BY_ROUND):
+                for ps in PASSES_BY_ROUND[n + 1]:
+                    regroup_weights(ps)

@@ -103,14 +103,24 @@ def tile_bilaterallstmcell_v_kernel(
         def load_chunk(n):
             b_tile, half = CHUNKS[n]
             rows = slice(b_tile * P, (b_tile + 1) * P)
-            cols = slice(half * K_PASS, (half + 1) * K_PASS)
             pre[n] = work.tile([P, N_GATES, K_PASS], F32, name="pre", bufs=3)
-            nc.sync.dma_start(out=pre[n][:], in_=gates[rows, :].rearrange("b (g h) -> b g h", g=N_GATES)[:, :, cols])
             given[n] = work.tile([P, 3, K_PASS], BF16, name="given", bufs=4)
+
+            def load_gate(gate):
+                first = gate * HIDDEN + half * K_PASS
+                nc.sync.dma_start(out=pre[n][:, gate, :], in_=gates[rows, first : first + K_PASS])
+
+            load_gate(GATE_I)
+            load_gate(GATE_C)
+            load_gate(GATE_F)
             nc.sync.dma_start(
                 out=given[n][:, 0, :], in_=hidden_memory_tm1[rows, HIDDEN + half * K_PASS : HIDDEN + (half + 1) * K_PASS]
             )
-            nc.sync.dma_start(out=given[n][:, 1:3, :], in_=grad_out[rows, :].rearrange("b (s h) -> b s h", s=2)[:, :, cols])
+            load_gate(GATE_O)
+            nc.sync.dma_start(
+                out=given[n][:, 1:3, :],
+                in_=grad_out[rows, :].rearrange("b (s h) -> b s h", s=2)[:, :, half * K_PASS : (half + 1) * K_PASS],
+            )
 
         def gate_values(n):
             sig[n] = work.tile([P, 3, K_PASS], F32, name="sig", bufs=3)
@@ -231,9 +241,9 @@ def tile_bilaterallstmcell_v_kernel(
         load_weights(1)
         make_identity(nc, ident[:])
         gate_values(0)
-        gate_values(1)
         products(0, nc.vector)
         cell_state(0)
+        gate_values(1)
         factors(0)
         for ps in PASSES_BY_ROUND[0]:
             regroup_weights(ps)

@@ -69,7 +69,7 @@ def tile_bilaterallstmcell_v_kernel(
         ident = keep.tile([P, P], F32)
 
         pre, given, sig, cand, cand_sq, prod = {}, {}, {}, {}, {}, {}
-        u_bank, dcs_bank, neg_tanh_c, tanh_c_sq, r_bank = {}, {}, {}, {}, {}
+        u_bank, dcs_bank, neg_tanh_c, tanh_c_sq, factor_bank = {}, {}, {}, {}, {}
         da_grouped, da_codes, da_scales, acc = {}, {}, {}, {}
 
         def load_weights(half):
@@ -172,16 +172,17 @@ def tile_bilaterallstmcell_v_kernel(
                 nc.tensor.transpose(out=dcs_bank[n][:, u, :], in_=dcs_words[:, u * P : (u + 1) * P], identity=ident[:])
 
         def factors(n):
-            r = work.tile([P, N_GATES, K_PASS], F32, name="r")
+            r = work.tile([P, 3, K_PASS], F32, name="r")
             nc.vector.scalar_tensor_tensor(
-                out=r[:, GATE_I : GATE_O + 1, :], in0=sig[n][:], scalar=1.0, in1=prod[n][:], op0=ALU.subtract, op1=ALU.mult
+                out=r[:, 0:2, :], in0=sig[n][:, GATE_I : GATE_F + 1, :], scalar=1.0, in1=prod[n][:, 0:2, :],
+                op0=ALU.subtract, op1=ALU.mult,
             )
             nc.vector.scalar_tensor_tensor(
-                out=r[:, GATE_C, :], in0=cand_sq[n][:], scalar=1.0, in1=sig[n][:, GATE_I, :], op0=ALU.subtract, op1=ALU.mult
+                out=r[:, 2, :], in0=cand_sq[n][:], scalar=1.0, in1=sig[n][:, GATE_I, :], op0=ALU.subtract, op1=ALU.mult
             )
-            r_bank[n] = {}
-            for gate in GATE_ORDER:
-                r_bank[n][gate] = transposed(r[:, gate, :], "r_bank")
+            factor_bank[n] = {GATE_O: transposed(sig[n][:, GATE_O, :], "o_bank")}
+            for j, gate in enumerate((GATE_I, GATE_F, GATE_C)):
+                factor_bank[n][gate] = transposed(r[:, j, :], "r_bank")
 
         def contract(n, gate):
             b_tile, half = CHUNKS[n]
@@ -210,9 +211,8 @@ def tile_bilaterallstmcell_v_kernel(
             nc.vector.scalar_tensor_tensor(
                 out=v[:], in0=tanh_c_sq[n][:], scalar=1.0, in1=value_last(u_bank[n][:]), op0=ALU.subtract, op1=ALU.mult
             )
-            nc.vector.tensor_tensor(
-                out=da_grouped[n][:, GATE_O], in0=value_last(r_bank[n][GATE_O][:]), in1=neg_tanh_c[n][:], op=ALU.mult
-            )
+            un = work.tile([P, P, PACK], F32, name="un")
+            nc.vector.tensor_tensor(out=un[:], in0=value_last(u_bank[n][:]), in1=neg_tanh_c[n][:], op=ALU.mult)
             neg_dc = work.tile([P, P, PACK], F32, name="neg_dc")
             nc.vector.tensor_tensor(
                 out=neg_dc[:].rearrange("p b (u e) -> p b u e", e=2),
@@ -220,10 +220,14 @@ def tile_bilaterallstmcell_v_kernel(
                 in1=dcs_bank[n][:].bitcast(BF16).rearrange("p u (b e) -> p b u e", e=2),
                 op=ALU.subtract,
             )
+            nc.vector.scalar_tensor_tensor(
+                out=da_grouped[n][:, GATE_O], in0=value_last(factor_bank[n][GATE_O][:]), scalar=1.0, in1=un[:],
+                op0=ALU.subtract, op1=ALU.mult,
+            )
             for k in range(1, N_GATES):
                 gate = GATE_ORDER[k]
                 nc.vector.tensor_tensor(
-                    out=da_grouped[n][:, gate], in0=value_last(r_bank[n][gate][:]), in1=neg_dc[:], op=ALU.mult
+                    out=da_grouped[n][:, gate], in0=value_last(factor_bank[n][gate][:]), in1=neg_dc[:], op=ALU.mult
                 )
                 if contract_at_once:
                     contract(n, GATE_ORDER[k - 1])

from contextlib import ExitStack

import concourse.mybir as mybir
from concourse.masks import make_identity

F32 = mybir.dt.float32
BF16 = mybir.dt.bfloat16
U32 = mybir.dt.uint32
U8 = mybir.dt.uint8
E4M3_X4 = mybir.dt.float8_e4m3fn_x4
E5M2_X4 = mybir.dt.float8_e5m2_x4
FUNC = mybir.ActivationFunctionType
ALU = mybir.AluOpType

P = 128
PACK = 4
K_PASS = P * PACK

BATCH, D_IN, HIDDEN = 512, 512, 1024
GATE_I, GATE_F, GATE_O, GATE_C = 0, 1, 2, 3
N_GATES = 4
GATE_ORDER = (GATE_O, GATE_I, GATE_F, GATE_C)
N_HALVES = HIDDEN // K_PASS
D_TILES = D_IN // P
CHUNKS = [(2 * pair + j, half) for pair in range(BATCH // P // 2) for half in range(N_HALVES) for j in range(2)]
N_CHUNKS = len(CHUNKS)
PASSES_BY_ROUND = (
    tuple(N_HALVES * gate for gate in GATE_ORDER),
    tuple(N_HALVES * gate + 1 for gate in GATE_ORDER[:2]),
    tuple(N_HALVES * gate + 1 for gate in GATE_ORDER[2:]),
)

FLOPS = 2 * BATCH * D_IN * N_GATES * HIDDEN
BYTES = 4 * BATCH * N_GATES * HIDDEN + 2 * BATCH * 3 * HIDDEN + 2 * D_IN * N_GATES * HIDDEN + 4 * BATCH * D_IN


def dram_order(ap):
    return ap.rearrange("p n (u q e) -> p (n u) e q", u=2, e=2)


def on_chip_order(ap):
    return ap.rearrange("p n (u e q) -> p (n u) e q", u=2, e=2)


def value_last(bank):
    return bank.rearrange("p t b -> p b t")


def tile_bilaterallstmcell_v_kernel(
    tc, x, hidden_memory_tm1, hidden_memory_tm2,
    Wi, Ui, Vi, Wf, Uf, Vf, Wo, Uo, Vo, Wc, Uc, Vc,
    gates, grad_out, out,
):
    nc = tc.nc
    weights = (Wi, Wf, Wo, Wc)

    with ExitStack() as stack:
        stack.enter_context(tc.manual_schedule())
        keep = stack.enter_context(tc.tile_pool(name="keep", bufs=1))
        work = stack.enter_context(tc.tile_pool(name="work", bufs=2))
        banks = stack.enter_context(tc.psum_pool(name="banks", bufs=6))
        sums = stack.enter_context(tc.psum_pool(name="sums", bufs=2))

        n_pass = N_GATES * N_HALVES
        w_rows = keep.tile([P, n_pass, D_TILES, K_PASS], BF16)
        w_grouped = keep.tile([P, n_pass, D_IN * PACK], BF16, align_bytes=64)
        w_codes = keep.tile([P, n_pass, D_IN], U32, align_bytes=64)
        w_scales = keep.tile([P, n_pass, D_IN], U8, align_bytes=64)
        ident = keep.tile([P, P], F32)

        pre, given, sig, cand, cand_sq, prod = {}, {}, {}, {}, {}, {}
        u_bank, dcs_bank, neg_tanh_c, tanh_c_sq, factor_bank = {}, {}, {}, {}, {}
        da_grouped, da_codes, da_scales, acc = {}, {}, {}, {}

        def load_weights(half):
            cols = slice(half * K_PASS, (half + 1) * K_PASS)
            for gate in GATE_ORDER:
                nc.sync.dma_start(
                    out=w_rows[:, N_HALVES * gate + half],
                    in_=weights[gate].rearrange("(j p) h -> p j h", p=P)[:, :, cols],
                )

        def regroup_weights(ps):
            words = w_rows[:, ps].bitcast(F32)
            grouped_words = w_grouped[:, ps].bitcast(F32).rearrange("p (d u) -> p d u", u=2)
            for d_half in range(2):
                bank = banks.tile([P, 2, 2 * P], F32, name="w_bank", tag="bank")
                for u in range(2):
                    for j in range(2):
                        nc.tensor.transpose(
                            out=bank[:, u, j * P : (j + 1) * P],
                            in_=words[:, 2 * d_half + j, u * P : (u + 1) * P],
                            identity=ident[:],
                        )
                nc.scalar.copy(
                    out=grouped_words[:, d_half * 2 * P : (d_half + 1) * 2 * P, :],
                    in_=bank[:].rearrange("p u d -> p d u"),
                )

        def quantise_weights(ps):
            nc.vector.quantize_mx(out=w_codes[:, ps].bitcast(E4M3_X4), scales=w_scales[:, ps], in_=w_grouped[:, ps])

        def load_chunk(n):
            b_tile, half = CHUNKS[n]
            rows = slice(b_tile * P, (b_tile + 1) * P)
            pre[n] = work.tile([P, N_GATES, K_PASS], F32, name="pre", bufs=3)
            given[n] = work.tile([P, 3, K_PASS], BF16, name="given", bufs=4)

            def load_gate(gate):
                first = gate * HIDDEN + half * K_PASS
                nc.sync.dma_start(out=pre[n][:, gate, :], in_=gates[rows, first : first + K_PASS])

            load_gate(GATE_I)
            load_gate(GATE_C)
            load_gate(GATE_F)
            nc.sync.dma_start(
                out=given[n][:, 0, :], in_=hidden_memory_tm1[rows, HIDDEN + half * K_PASS : HIDDEN + (half + 1) * K_PASS]
            )
            load_gate(GATE_O)
            nc.sync.dma_start(
                out=given[n][:, 1:3, :],
                in_=grad_out[rows, :].rearrange("b (s h) -> b s h", s=2)[:, :, half * K_PASS : (half + 1) * K_PASS],
            )

        def gate_values(n):
            sig[n] = work.tile([P, 3, K_PASS], F32, name="sig", bufs=3)
            cand[n] = work.tile([P, 1, K_PASS], F32, name="cand", bufs=3)
            cand_sq[n] = work.tile([P, K_PASS], F32, name="cand_sq", bufs=3)

            def sigmoid(gate):
                nc.scalar.activation(
                    out=on_chip_order(sig[n][:, gate : gate + 1, :]), in_=dram_order(pre[n][:, gate : gate + 1, :]), func=FUNC.Sigmoid
                )

            sigmoid(GATE_I)
            nc.scalar.activation(
                out=on_chip_order(cand[n][:]), in_=dram_order(pre[n][:, GATE_C : GATE_C + 1, :]), func=FUNC.Tanh
            )
            sigmoid(GATE_F)
            sigmoid(GATE_O)
            nc.scalar.activation(out=cand_sq[n][:], in_=cand[n][:, 0, :], func=FUNC.Square)

        def products(n, engine):
            prod[n] = work.tile([P, 3, K_PASS], F32, name="prod", bufs=1)
            engine.tensor_tensor(out=prod[n][:, 0, :], in0=sig[n][:, GATE_I, :], in1=cand[n][:, 0, :], op=ALU.mult)
            for j, gate in ((1, GATE_F), (2, GATE_O)):
                engine.tensor_tensor(
                    out=on_chip_order(prod[n][:, j : j + 1, :]), in0=on_chip_order(sig[n][:, gate : gate + 1, :]),
                    in1=dram_order(given[n][:, j - 1 : j, :]), op=ALU.mult,
                )

        def transposed(rows_ap, name):
            bank = banks.tile([P, PACK, P], F32, name=name, tag="bank")
            for t in range(PACK):
                nc.tensor.transpose(out=bank[:, t, :], in_=rows_ap[:, t * P : (t + 1) * P], identity=ident[:])
            return bank

        def cell_state(n):
            cell_bank = banks.tile([P, PACK, P], F32, name="cell_bank", tag="bank")
            for t in range(PACK):
                block = slice(t * P, (t + 1) * P)
                nc.tensor.matmul(out=cell_bank[:, t, :], lhsT=prod[n][:, 0, block], rhs=ident[:], is_transpose=True, start=True, stop=False)
                nc.tensor.matmul(out=cell_bank[:, t, :], lhsT=prod[n][:, 1, block], rhs=ident[:], is_transpose=True, start=False, stop=True)
            neg_tanh_c[n] = work.tile([P, P, PACK], F32, name="neg_tanh_c")
            nc.scalar.activation(out=neg_tanh_c[n][:], in_=value_last(cell_bank[:]), func=FUNC.Tanh, scale=-1.0)
            tanh_c_sq[n] = work.tile([P, P, PACK], F32, name="tanh_c_sq")
            nc.scalar.activation(out=tanh_c_sq[n][:], in_=neg_tanh_c[n][:], func=FUNC.Square)
            u_bank[n] = transposed(prod[n][:, 2, :], "u_bank")
            dcs_words = given[n][:, 2, :].bitcast(F32)
            dcs_bank[n] = banks.tile([P, 2, P], F32, name="dcs_bank", tag="bank")
            for u in range(2):
                nc.tensor.transpose(out=dcs_bank[n][:, u, :], in_=dcs_words[:, u * P : (u + 1) * P], identity=ident[:])

        def factors(n):
            r = work.tile([P, 3, K_PASS], F32, name="r")
            nc.vector.scalar_tensor_tensor(
                out=r[:, 0:2, :], in0=sig[n][:, GATE_I : GATE_F + 1, :], scalar=1.0, in1=prod[n][:, 0:2, :],
                op0=ALU.subtract, op1=ALU.mult,
            )
            nc.vector.scalar_tensor_tensor(
                out=r[:, 2, :], in0=cand_sq[n][:], scalar=1.0, in1=sig[n][:, GATE_I, :], op0=ALU.subtract, op1=ALU.mult
            )
            factor_bank[n] = {GATE_O: transposed(sig[n][:, GATE_O, :], "o_bank")}
            for j, gate in enumerate((GATE_I, GATE_F, GATE_C)):
                factor_bank[n][gate] = transposed(r[:, j, :], "r_bank")

        def contract(n, gate):
            b_tile, half = CHUNKS[n]
            nc.vector.quantize_mx(
                out=da_codes[n][:, gate].bitcast(E5M2_X4),
                scales=da_scales[n][:, gate],
                in_=da_grouped[n][:, gate].rearrange("p b t -> p (b t)"),
            )
            ps = N_HALVES * gate + half
            nc.tensor.matmul_mx(
                out=acc[b_tile][:],
                lhsT=da_codes[n][:, gate].bitcast(E5M2_X4), lhsT_scale=da_scales[n][:, gate],
                rhs=w_codes[:, ps].bitcast(E4M3_X4), rhs_scale=w_scales[:, ps],
                start=(half == 0 and gate == GATE_ORDER[0]),
                stop=(half == N_HALVES - 1 and gate == GATE_ORDER[-1]),
            )

        def gradients(n, contract_at_once):
            b_tile, half = CHUNKS[n]
            da_grouped[n] = work.tile([P, N_GATES, P, PACK], BF16, name="da_grouped", align_bytes=64)
            da_codes[n] = work.tile([P, N_GATES, P], U32, name="da_codes", align_bytes=64)
            da_scales[n] = work.tile([P, N_GATES, P], U8, name="da_scales", align_bytes=64)
            if half == 0:
                acc[b_tile] = sums.tile([P, D_IN], F32, name="acc")
            v = work.tile([P, P, PACK], F32, name="v")
            nc.vector.scalar_tensor_tensor(
                out=v[:], in0=tanh_c_sq[n][:], scalar=1.0, in1=value_last(u_bank[n][:]), op0=ALU.subtract, op1=ALU.mult
            )
            un = work.tile([P, P, PACK], F32, name="un")
            nc.vector.tensor_tensor(out=un[:], in0=value_last(u_bank[n][:]), in1=neg_tanh_c[n][:], op=ALU.mult)
            neg_dc = work.tile([P, P, PACK], F32, name="neg_dc")
            nc.vector.tensor_tensor(
                out=neg_dc[:].rearrange("p b (u e) -> p b u e", e=2),
                in0=v[:].rearrange("p b (u e) -> p b u e", e=2),
                in1=dcs_bank[n][:].bitcast(BF16).rearrange("p u (b e) -> p b u e", e=2),
                op=ALU.subtract,
            )
            nc.vector.scalar_tensor_tensor(
                out=da_grouped[n][:, GATE_O], in0=value_last(factor_bank[n][GATE_O][:]), scalar=1.0, in1=un[:],
                op0=ALU.subtract, op1=ALU.mult,
            )
            for k in range(1, N_GATES):
                gate = GATE_ORDER[k]
                nc.vector.tensor_tensor(
                    out=da_grouped[n][:, gate], in0=value_last(factor_bank[n][gate][:]), in1=neg_dc[:], op=ALU.mult
                )
                if contract_at_once:
                    contract(n, GATE_ORDER[k - 1])

        def store(b_tile):
            result = work.tile([P, D_IN], F32, name="result")
            nc.scalar.copy(out=result[:], in_=acc[b_tile][:])
            nc.sync.dma_start(out=out[b_tile * P : (b_tile + 1) * P, :], in_=result[:])

        load_chunk(0)
        load_chunk(1)
        load_weights(0)
        load_chunk(2)
        load_chunk(3)
        load_weights(1)
        make_identity(nc, ident[:])
        gate_values(0)
        products(0, nc.vector)
        cell_state(0)
        gate_values(1)
        factors(0)
        for ps in PASSES_BY_ROUND[0]:
            regroup_weights(ps)
        gate_values(2)

        for n in range(N_CHUNKS):
            if n + 4 < N_CHUNKS:
                load_chunk(n + 4)
            if n + 1 < N_CHUNKS:
                products(n + 1, nc.gpsimd)
                cell_state(n + 1)
            if n + 3 < N_CHUNKS:
                gate_values(n + 3)
            last_round = n == N_CHUNKS - 1
            gradients(n, contract_at_once=last_round)
            if n < len(PASSES_BY_ROUND):
                for ps in PASSES_BY_ROUND[n]:
                    quantise_weights(ps)
            for gate in GATE_ORDER[-1:] if last_round else GATE_ORDER:
                contract(n, gate)
            if CHUNKS[n][1] == N_HALVES - 1:
                store(CHUNKS[n][0])
            if n + 1 < N_CHUNKS:
                factors(n + 1)
            if n + 1 < len(PASSES_BY_ROUND):
                for ps in PASSES_BY_ROUND[n + 1]:
                    regroup_weights(ps)
